import numpy as np
import ml_dtypes


def mxq(x, axis, fmt="e4m3"):
    dtype, down = {"e4m3": (ml_dtypes.float8_e4m3fn, 7), "e5m2": (ml_dtypes.float8_e5m2, 14)}[fmt]
    v = np.moveaxis(np.asarray(x, np.float32).astype(ml_dtypes.bfloat16).astype(np.float64), axis, -1)
    blocks = v.reshape(v.shape[:-1] + (-1, 32))
    amax = np.abs(blocks).max(-1, keepdims=True)
    byte = np.maximum(np.where(amax > 0, np.frexp(amax)[1] - 1 + 127, 0) - down, 1)
    scale = np.exp2(byte - 127.0)
    codes = (blocks / scale).astype(np.float32).astype(dtype).astype(np.float64)
    return np.moveaxis((codes * scale).reshape(v.shape), -1, axis)


WIDE = False


def mx_kscale(k):
    if not WIDE:
        return np.ones(k)
    levels = np.array([10, -10, 5, -5, 0])
    a = np.random.permutation(np.resize(levels, k // 512 * 4)).reshape(k // 512, 4)
    idx = np.arange(k)
    return np.exp2(a[idx // 512, idx % 128 // 32])


BF16 = ml_dtypes.bfloat16


def bf(x):
    return np.asarray(x, np.float32).astype(BF16)


def f64(x):
    return np.asarray(x).astype(np.float64)


E2M1 = np.array([0.0, 0.5, 1.0, 1.5, 2.0, 3.0, 4.0, 6.0, -0.0, -0.5, -1.0, -1.5, -2.0, -3.0, -4.0, -6.0])


def pack_weight(w, fmt):
    k, n = w.shape
    w = f64(bf(w)).reshape(k // 32, 32, n)
    amax = np.abs(w).max(1)
    if fmt == "e4m3":
        byte = np.frexp(amax)[1] - 1 + 127 - 7
    else:
        mant, ex = np.frexp(amax / 6.0)
        byte = np.where(mant > 0.5, ex, ex - 1) + 127
    byte = np.clip(np.where(amax > 0, byte, 1), 1, 254)
    scaled = (w * np.exp2(127.0 - byte)[:, None, :]).reshape(k, n).astype(np.float32)
    by_word = np.ascontiguousarray(scaled.reshape(k // 512, 128, 4, n).transpose(0, 1, 3, 2))
    if fmt == "e4m3":
        words = by_word.astype(ml_dtypes.float8_e4m3fn).view(np.uint8)
    else:
        c = by_word.astype(ml_dtypes.float4_e2m1fn).view(np.uint8) & 0xF
        words = c[..., 0::2] | (c[..., 1::2] << 4)
    return np.ascontiguousarray(words), np.ascontiguousarray(byte.astype(np.uint8).reshape(k // 512, 16, n))


def unpack_weight(words, scales, fmt):
    g, p, n, _ = words.shape
    if fmt == "e4m3":
        vals = np.ascontiguousarray(words).view(ml_dtypes.float8_e4m3fn).astype(np.float64)
    else:
        nib = np.empty((g, p, n, 4), np.uint8)
        nib[..., 0::2] = words & 0xF
        nib[..., 1::2] = words >> 4
        vals = E2M1[nib]
    vals = vals * np.repeat(np.exp2(scales.astype(np.float64) - 127.0), 8, axis=1)[..., None]
    return vals.transpose(0, 1, 3, 2).reshape(g * 512, n)

def pack4(w):
    words, scales = pack_weight(w, "e2m1")
    return words.reshape(words.shape[0], 128, -1), scales


def unpack4(words, scales):
    return unpack_weight(words.reshape(words.shape[0], 128, -1, 2), scales, "e2m1")


B, H, L, G, P = 128, 512, 4, 4, 2


def sigmoid(v):
    return 1.0 / (1.0 + np.exp(-v))


def setup_inputs():
    s, t = mx_kscale(H), mx_kscale(H)
    sc = 1.0 / np.sqrt(H)
    lstm_input = bf(np.random.standard_normal((B, H)) * 0.5 * s)
    h_prev = bf(np.random.standard_normal((B, H)) * t)
    c_prev = bf(np.random.standard_normal((B, H)))
    w_ih = np.random.standard_normal((G * H, H)) * sc / s[None, :]
    w_hh = np.random.standard_normal((G * H, H)) * sc / t[None, :]
    b_ih = bf(np.random.standard_normal(G * H) * 0.3)
    b_hh = bf(np.random.standard_normal(G * H) * 0.3)
    w_ih_words, w_ih_scales = pack4(np.ascontiguousarray(w_ih.T))
    w_hh_words, w_hh_scales = pack4(np.ascontiguousarray(w_hh.T))
    return {"lstm_input": lstm_input,
            "h_prev": h_prev,
            "c_prev": c_prev,
            "w_ih_words": w_ih_words,
            "w_ih_scales": w_ih_scales,
            "w_hh_words": w_hh_words,
            "w_hh_scales": w_hh_scales,
            "b_ih": b_ih,
            "b_hh": b_hh}


def reference(lstm_input, h_prev, c_prev, w_ih_words, w_ih_scales, w_hh_words, w_hh_scales, b_ih, b_hh):
    gates = ((mxq(f64(lstm_input), 1, "e4m3") @ unpack4(w_ih_words, w_ih_scales)) + f64(b_ih)
             + (mxq(f64(h_prev), 1, "e4m3") @ unpack4(w_hh_words, w_hh_scales)) + f64(b_hh))
    i, f, g, o = np.split(gates, G, axis=-1)
    i = sigmoid(i)
    f = sigmoid(f)
    g = np.tanh(g)
    o = sigmoid(o)
    c_next = f * f64(c_prev) + i * g
    h_next = o * np.tanh(c_next)
    return h_next, c_next

@@ -1,0 +1,193 @@
+from contextlib import ExitStack
+
+import concourse.mybir as mybir
+from concourse.masks import make_identity
+
+F32 = mybir.dt.float32
+BF16 = mybir.dt.bfloat16
+I32 = mybir.dt.int32
+U32 = mybir.dt.uint32
+U8 = mybir.dt.uint8
+FP8X4 = mybir.dt.float8_e4m3fn_x4
+FP4X4 = mybir.dt.float4_e2m1fn_x4
+ACT = mybir.ActivationFunctionType
+ALU = mybir.AluOpType
+
+P = 128
+HIDDEN = 512
+GATES = 4
+BLOCKS = HIDDEN // P
+COLUMNS = GATES * HIDDEN
+FP4_WORD_BYTES = 2
+QUADRANTS = 4
+TAIL_BLOCKS = 2
+
+GATE_I, GATE_F, GATE_G, GATE_O = 0, 1, 2, 3
+
+FLOPS = 2 * P * (2 * HIDDEN) * COLUMNS
+
+
+def load_scale_plane(nc, plane, scales):
+    rows = scales[0].rearrange("(quadrant r) n -> r quadrant n", r=4)
+    for r in range(4):
+        nc.sync.dma_start(out=plane[r:P:32, :].bitcast(I32), in_=rows[r].bitcast(I32))
+
+
+def load_gate_words(nc, words_sb, words, g):
+    cols = slice(g * HIDDEN * FP4_WORD_BYTES, (g + 1) * HIDDEN * FP4_WORD_BYTES)
+    nc.sync.dma_start(out=words_sb[:, cols].bitcast(I32), in_=words[0][:, cols].bitcast(I32))
+
+
+def transpose_words(nc, bank, rows_sb, ident_f32):
+    words = rows_sb[:].bitcast(F32)
+    for u in range(2):
+        nc.tensor.transpose(bank[:, u, :], words[:, u : HIDDEN // 2 : 2], ident_f32[:])
+
+
+def tile_multilayerlstmcell_pa_s_kernel(
+    tc, lstm_input, h_prev, c_prev, w_ih_words, w_ih_scales, w_hh_words, w_hh_scales, b_ih, b_hh, out_0, out_1
+):
+    nc = tc.nc
+    gate_order = (GATE_F, GATE_I, GATE_G, GATE_O)
+    with ExitStack() as ctx:
+        keep = ctx.enter_context(tc.tile_pool(name="keep", bufs=1))
+        psum_small = ctx.enter_context(tc.psum_pool(name="psum_small", bufs=4))
+        psum_gates = ctx.enter_context(tc.psum_pool(name="psum_gates", bufs=GATES))
+        ctx.enter_context(tc.manual_schedule())
+
+        x_sb = keep.tile([P, HIDDEN], BF16)
+        h_sb = keep.tile([P, HIDDEN], BF16)
+        c_sb = keep.tile([P, HIDDEN], BF16)
+        w_ih_sb = keep.tile([P, COLUMNS * FP4_WORD_BYTES], U8, align_bytes=64)
+        w_hh_sb = keep.tile([P, COLUMNS * FP4_WORD_BYTES], U8, align_bytes=64)
+        w_ih_plane = keep.tile([P, COLUMNS], U8, align_bytes=64)
+        w_hh_plane = keep.tile([P, COLUMNS], U8, align_bytes=64)
+        bias_rows = keep.tile([P, P], BF16)
+        ident_f32 = keep.tile([P, P], F32)
+        ident_bf16 = keep.tile([P, P], BF16)
+        table_warm = keep.tile([P, 2], F32)
+
+        nc.vector.memset(w_ih_plane[:].bitcast(I32), 0)
+        nc.vector.memset(table_warm[:], 0.0)
+        nc.vector.memset(w_hh_plane[:].bitcast(I32), 0)
+
+        load_scale_plane(nc, w_ih_plane, w_ih_scales)
+        nc.scalar.dma_start(out=x_sb[:], in_=lstm_input)
+        nc.scalar.dma_start(out=h_sb[:], in_=h_prev)
+        load_gate_words(nc, w_ih_sb, w_ih_words, gate_order[0])
+        load_gate_words(nc, w_hh_sb, w_hh_words, gate_order[0])
+        load_scale_plane(nc, w_hh_plane, w_hh_scales)
+        for g in gate_order[1:]:
+            load_gate_words(nc, w_ih_sb, w_ih_words, g)
+            load_gate_words(nc, w_hh_sb, w_hh_words, g)
+
+        nc.gpsimd.memset(bias_rows[:], 0.0)
+        nc.gpsimd.dma_start(out=bias_rows[0:16, :], in_=b_ih.rearrange("(m p) -> m p", p=P))
+        nc.gpsimd.dma_start(out=bias_rows[16:32, :], in_=b_hh.rearrange("(m p) -> m p", p=P))
+        make_identity(nc, ident_f32[:])
+        nc.gpsimd.dma_start(out=c_sb[:], in_=c_prev)
+        nc.vector.tensor_copy(out=ident_bf16[:], in_=ident_f32[:])
+
+        nc.scalar.activation(out=table_warm[:, 1:2], in_=table_warm[:, 0:1], func=ACT.Sigmoid)
+
+        x_bank = psum_small.tile([P, 2, P], F32, tag="small")
+        h_bank = psum_small.tile([P, 2, P], F32, tag="small")
+        transpose_words(nc, x_bank, x_sb, ident_f32)
+        transpose_words(nc, h_bank, h_sb, ident_f32)
+
+        x_grouped = keep.tile([P, P, 4], BF16, align_bytes=64)
+        h_grouped = keep.tile([P, P, 4], BF16, align_bytes=64)
+        nc.vector.tensor_copy(
+            out=x_grouped[:].rearrange("p b t -> p (b t)").bitcast(F32).rearrange("p (b u) -> p b u", u=2),
+            in_=x_bank[:].rearrange("p u b -> p b u"),
+        )
+        nc.scalar.copy(
+            out=h_grouped[:].rearrange("p b t -> p (b t)").bitcast(F32).rearrange("p (b u) -> p b u", u=2),
+            in_=h_bank[:].rearrange("p u b -> p b u"),
+        )
+        x_codes = keep.tile([P, P], U32, align_bytes=64)
+        h_codes = keep.tile([P, P], U32, align_bytes=64)
+        x_plane = keep.tile([P, P], U8, align_bytes=64)
+        h_plane = keep.tile([P, P], U8, align_bytes=64)
+        nc.vector.quantize_mx(
+            out=x_codes[:].bitcast(FP8X4), scales=x_plane[:], in_=x_grouped[:].rearrange("p b t -> p (b t)")
+        )
+        nc.vector.quantize_mx(
+            out=h_codes[:].bitcast(FP8X4), scales=h_plane[:], in_=h_grouped[:].rearrange("p b t -> p (b t)")
+        )
+
+        bias_bank = psum_small.tile([P, P], BF16, tag="small")
+        nc.tensor.transpose(bias_bank[:], bias_rows[:], ident_bf16[:])
+        bias = keep.tile([P, GATES * BLOCKS], F32)
+        nc.vector.tensor_reduce(
+            out=bias[:],
+            in_=bias_bank[:, 0 : 2 * GATES * BLOCKS].rearrange("p (s m) -> p m s", s=2),
+            axis=mybir.AxisListType.X,
+            op=ALU.add,
+        )
+
+        gate_func = {GATE_I: ACT.Sigmoid, GATE_F: ACT.Sigmoid, GATE_G: ACT.Tanh, GATE_O: ACT.Sigmoid}
+        gate = {}
+        for g in gate_order:
+            acc = psum_gates.tile([P, BLOCKS, P], F32, tag="acc")
+            for j in range(BLOCKS):
+                m = g * BLOCKS + j
+                word_cols = slice(m * P * FP4_WORD_BYTES, (m + 1) * P * FP4_WORD_BYTES)
+                scale_cols = slice(m * P, (m + 1) * P)
+                nc.tensor.matmul_mx(
+                    out=acc[:, j, :],
+                    lhsT=w_ih_sb[:, word_cols].bitcast(FP4X4),
+                    lhsT_scale=w_ih_plane[:, scale_cols],
+                    rhs=x_codes[:].bitcast(FP8X4),
+                    rhs_scale=x_plane[:],
+                    start=True,
+                    stop=False,
+                )
+                nc.tensor.matmul_mx(
+                    out=acc[:, j, :],
+                    lhsT=w_hh_sb[:, word_cols].bitcast(FP4X4),
+                    lhsT_scale=w_hh_plane[:, scale_cols],
+                    rhs=h_codes[:].bitcast(FP8X4),
+                    rhs_scale=h_plane[:],
+                    start=False,
+                    stop=True,
+                )
+            gate[g] = keep.tile([P, BLOCKS, P], F32, name="gate%d" % g)
+            for j in range(BLOCKS):
+                m = g * BLOCKS + j
+                nc.scalar.activation(
+                    out=gate[g][:, j, :], in_=acc[:, j, :], func=gate_func[g], bias=bias[:, m : m + 1], scale=1.0
+                )
+
+        def transpose_back(source_t, first, count):
+            bank = psum_small.tile([P, count * P], F32, tag="small", name="back")
+            for n in range(count):
+                nc.tensor.transpose(bank[:, n * P : (n + 1) * P], source_t[:, first + n, :], ident_f32[:])
+            return bank
+
+        input_g_t = keep.tile([P, BLOCKS, P], F32)
+        forget_c = keep.tile([P, HIDDEN], F32)
+        c_next = keep.tile([P, HIDDEN], F32)
+        tanh_c = keep.tile([P, HIDDEN], F32)
+        h_next = keep.tile([P, HIDDEN], F32)
+        chunk_starts = list(range(0, BLOCKS, TAIL_BLOCKS))
+
+        f_bank = transpose_back(gate[GATE_F], 0, BLOCKS)
+        input_g_banks = []
+        for first in chunk_starts:
+            blocks = slice(first, first + TAIL_BLOCKS)
+            nc.vector.tensor_tensor(
+                out=input_g_t[:, blocks, :], in0=gate[GATE_I][:, blocks, :], in1=gate[GATE_G][:, blocks, :], op=ALU.mult
+            )
+            input_g_banks.append(transpose_back(input_g_t, first, TAIL_BLOCKS))
+        nc.vector.tensor_tensor(out=forget_c[:], in0=f_bank[:], in1=c_sb[:], op=ALU.mult)
+        for first, bank in zip(chunk_starts, input_g_banks):
+            cols = slice(first * P, (first + TAIL_BLOCKS) * P)
+            nc.vector.tensor_tensor(out=c_next[:, cols], in0=bank[:], in1=forget_c[:, cols], op=ALU.add)
+            nc.sync.dma_start(out=out_1[:, cols], in_=c_next[:, cols])
+            nc.scalar.activation(out=tanh_c[:, cols], in_=c_next[:, cols], func=ACT.Tanh)
+        for first in chunk_starts:
+            cols = slice(first * P, (first + TAIL_BLOCKS) * P)
+            o_bank = transpose_back(gate[GATE_O], first, TAIL_BLOCKS)
+            nc.vector.tensor_tensor(out=h_next[:, cols], in0=o_bank[:], in1=tanh_c[:, cols], op=ALU.mult)
+            nc.sync.dma_start(out=out_0[:, cols], in_=h_next[:, cols])

@@ -19,7 +19,7 @@ GATES = 4
 BLOCKS = HIDDEN // P
 COLUMNS = GATES * HIDDEN
 FP4_WORD_BYTES = 2
-QUADRANTS = 4
+BANK_BLOCKS = 2
 TAIL_BLOCKS = 2
 
 GATE_I, GATE_F, GATE_G, GATE_O = 0, 1, 2, 3
@@ -33,8 +33,9 @@ def load_scale_plane(nc, plane, scales):
         nc.sync.dma_start(out=plane[r:P:32, :].bitcast(I32), in_=rows[r].bitcast(I32))
 
 
-def load_gate_words(nc, words_sb, words, g):
-    cols = slice(g * HIDDEN * FP4_WORD_BYTES, (g + 1) * HIDDEN * FP4_WORD_BYTES)
+def load_words(nc, words_sb, words, half):
+    half_bytes = COLUMNS * FP4_WORD_BYTES // 2
+    cols = slice(half * half_bytes, (half + 1) * half_bytes)
     nc.sync.dma_start(out=words_sb[:, cols].bitcast(I32), in_=words[0][:, cols].bitcast(I32))
 
 
@@ -67,6 +68,8 @@ def tile_multilayerlstmcell_pa_s_kernel(
         ident_bf16 = keep.tile([P, P], BF16)
         table_warm = keep.tile([P, 2], F32)
 
+        nc.vector.memset(bias_rows[:], 0.0)
+        nc.vector.memset(ident_f32[:], 0.0)
         nc.vector.memset(w_ih_plane[:].bitcast(I32), 0)
         nc.vector.memset(table_warm[:], 0.0)
         nc.vector.memset(w_hh_plane[:].bitcast(I32), 0)
@@ -74,17 +77,15 @@ def tile_multilayerlstmcell_pa_s_kernel(
         load_scale_plane(nc, w_ih_plane, w_ih_scales)
         nc.scalar.dma_start(out=x_sb[:], in_=lstm_input)
         nc.scalar.dma_start(out=h_sb[:], in_=h_prev)
-        load_gate_words(nc, w_ih_sb, w_ih_words, gate_order[0])
-        load_gate_words(nc, w_hh_sb, w_hh_words, gate_order[0])
+        load_words(nc, w_ih_sb, w_ih_words, 0)
+        load_words(nc, w_hh_sb, w_hh_words, 0)
         load_scale_plane(nc, w_hh_plane, w_hh_scales)
-        for g in gate_order[1:]:
-            load_gate_words(nc, w_ih_sb, w_ih_words, g)
-            load_gate_words(nc, w_hh_sb, w_hh_words, g)
+        load_words(nc, w_ih_sb, w_ih_words, 1)
+        load_words(nc, w_hh_sb, w_hh_words, 1)
 
-        nc.gpsimd.memset(bias_rows[:], 0.0)
         nc.gpsimd.dma_start(out=bias_rows[0:16, :], in_=b_ih.rearrange("(m p) -> m p", p=P))
         nc.gpsimd.dma_start(out=bias_rows[16:32, :], in_=b_hh.rearrange("(m p) -> m p", p=P))
-        make_identity(nc, ident_f32[:])
+        make_identity(nc, ident_f32[:], nomemset=True)
         nc.gpsimd.dma_start(out=c_sb[:], in_=c_prev)
         nc.vector.tensor_copy(out=ident_bf16[:], in_=ident_f32[:])
 
@@ -126,53 +127,60 @@ def tile_multilayerlstmcell_pa_s_kernel(
             op=ALU.add,
         )
 
-        gate_func = {GATE_I: ACT.Sigmoid, GATE_F: ACT.Sigmoid, GATE_G: ACT.Tanh, GATE_O: ACT.Sigmoid}
-        gate = {}
-        for g in gate_order:
-            acc = psum_gates.tile([P, BLOCKS, P], F32, tag="acc")
-            for j in range(BLOCKS):
-                m = g * BLOCKS + j
-                word_cols = slice(m * P * FP4_WORD_BYTES, (m + 1) * P * FP4_WORD_BYTES)
-                scale_cols = slice(m * P, (m + 1) * P)
-                nc.tensor.matmul_mx(
-                    out=acc[:, j, :],
-                    lhsT=w_ih_sb[:, word_cols].bitcast(FP4X4),
-                    lhsT_scale=w_ih_plane[:, scale_cols],
-                    rhs=x_codes[:].bitcast(FP8X4),
-                    rhs_scale=x_plane[:],
-                    start=True,
-                    stop=False,
-                )
-                nc.tensor.matmul_mx(
-                    out=acc[:, j, :],
-                    lhsT=w_hh_sb[:, word_cols].bitcast(FP4X4),
-                    lhsT_scale=w_hh_plane[:, scale_cols],
-                    rhs=h_codes[:].bitcast(FP8X4),
-                    rhs_scale=h_plane[:],
-                    start=False,
-                    stop=True,
-                )
-            gate[g] = keep.tile([P, BLOCKS, P], F32, name="gate%d" % g)
-            for j in range(BLOCKS):
-                m = g * BLOCKS + j
-                nc.scalar.activation(
-                    out=gate[g][:, j, :], in_=acc[:, j, :], func=gate_func[g], bias=bias[:, m : m + 1], scale=1.0
-                )
-
         def transpose_back(source_t, first, count):
             bank = psum_small.tile([P, count * P], F32, tag="small", name="back")
             for n in range(count):
                 nc.tensor.transpose(bank[:, n * P : (n + 1) * P], source_t[:, first + n, :], ident_f32[:])
             return bank
 
-        input_g_t = keep.tile([P, BLOCKS, P], F32)
+        gate_func = {GATE_I: ACT.Sigmoid, GATE_F: ACT.Sigmoid, GATE_G: ACT.Tanh, GATE_O: ACT.Sigmoid}
+        gate = {}
         forget_c = keep.tile([P, HIDDEN], F32)
+        for g in gate_order:
+            if g == GATE_O:
+                f_bank = transpose_back(gate[GATE_F], 0, BLOCKS)
+                nc.vector.tensor_tensor(out=forget_c[:], in0=f_bank[:], in1=c_sb[:], op=ALU.mult)
+            gate[g] = keep.tile([P, BLOCKS, P], F32, name="gate%d" % g)
+            for first in range(0, BLOCKS, BANK_BLOCKS):
+                acc = psum_gates.tile([P, BANK_BLOCKS, P], F32, tag="acc")
+                for n in range(BANK_BLOCKS):
+                    m = g * BLOCKS + first + n
+                    word_cols = slice(m * P * FP4_WORD_BYTES, (m + 1) * P * FP4_WORD_BYTES)
+                    scale_cols = slice(m * P, (m + 1) * P)
+                    nc.tensor.matmul_mx(
+                        out=acc[:, n, :],
+                        lhsT=w_ih_sb[:, word_cols].bitcast(FP4X4),
+                        lhsT_scale=w_ih_plane[:, scale_cols],
+                        rhs=x_codes[:].bitcast(FP8X4),
+                        rhs_scale=x_plane[:],
+                        start=True,
+                        stop=False,
+                    )
+                    nc.tensor.matmul_mx(
+                        out=acc[:, n, :],
+                        lhsT=w_hh_sb[:, word_cols].bitcast(FP4X4),
+                        lhsT_scale=w_hh_plane[:, scale_cols],
+                        rhs=h_codes[:].bitcast(FP8X4),
+                        rhs_scale=h_plane[:],
+                        start=False,
+                        stop=True,
+                    )
+                for n in range(BANK_BLOCKS):
+                    m = g * BLOCKS + first + n
+                    nc.scalar.activation(
+                        out=gate[g][:, first + n, :],
+                        in_=acc[:, n, :],
+                        func=gate_func[g],
+                        bias=bias[:, m : m + 1],
+                        scale=1.0,
+                    )
+
+        input_g_t = keep.tile([P, BLOCKS, P], F32)
         c_next = keep.tile([P, HIDDEN], F32)
         tanh_c = keep.tile([P, HIDDEN], F32)
         h_next = keep.tile([P, HIDDEN], F32)
         chunk_starts = list(range(0, BLOCKS, TAIL_BLOCKS))
 
-        f_bank = transpose_back(gate[GATE_F], 0, BLOCKS)
         input_g_banks = []
         for first in chunk_starts:
             blocks = slice(first, first + TAIL_BLOCKS)
@@ -180,7 +188,6 @@ def tile_multilayerlstmcell_pa_s_kernel(
                 out=input_g_t[:, blocks, :], in0=gate[GATE_I][:, blocks, :], in1=gate[GATE_G][:, blocks, :], op=ALU.mult
             )
             input_g_banks.append(transpose_back(input_g_t, first, TAIL_BLOCKS))
-        nc.vector.tensor_tensor(out=forget_c[:], in0=f_bank[:], in1=c_sb[:], op=ALU.mult)
         for first, bank in zip(chunk_starts, input_g_banks):
             cols = slice(first * P, (first + TAIL_BLOCKS) * P)
             nc.vector.tensor_tensor(out=c_next[:, cols], in0=bank[:], in1=forget_c[:, cols], op=ALU.add)

@@ -19,7 +19,8 @@ GATES = 4
 BLOCKS = HIDDEN // P
 COLUMNS = GATES * HIDDEN
 FP4_WORD_BYTES = 2
-BANK_BLOCKS = 2
+WARM_PASSES_EARLY = 4
+WARM_PASSES_GAP = 2
 TAIL_BLOCKS = 2
 
 GATE_I, GATE_F, GATE_G, GATE_O = 0, 1, 2, 3
@@ -33,10 +34,14 @@ def load_scale_plane(nc, plane, scales):
         nc.sync.dma_start(out=plane[r:P:32, :].bitcast(I32), in_=rows[r].bitcast(I32))
 
 
-def load_words(nc, words_sb, words, half):
-    half_bytes = COLUMNS * FP4_WORD_BYTES // 2
-    cols = slice(half * half_bytes, (half + 1) * half_bytes)
+def load_gate_words(nc, words_sb, words, g):
+    cols = slice(g * HIDDEN * FP4_WORD_BYTES, (g + 1) * HIDDEN * FP4_WORD_BYTES)
     nc.sync.dma_start(out=words_sb[:, cols].bitcast(I32), in_=words[0][:, cols].bitcast(I32))
+
+
+def warm_tensor_engine(nc, bank, zeros, passes):
+    for n in range(passes):
+        nc.tensor.matmul(out=bank[:], lhsT=zeros[:], rhs=zeros[:], start=True, stop=True)
 
 
 def transpose_words(nc, bank, rows_sb, ident_f32):
@@ -67,9 +72,12 @@ def tile_multilayerlstmcell_pa_s_kernel(
         ident_f32 = keep.tile([P, P], F32)
         ident_bf16 = keep.tile([P, P], BF16)
         table_warm = keep.tile([P, 2], F32)
+        zeros = keep.tile([P, P], F32)
 
-        nc.vector.memset(bias_rows[:], 0.0)
-        nc.vector.memset(ident_f32[:], 0.0)
+        nc.vector.memset(zeros[:], 0.0)
+        warm_bank = psum_small.tile([P, P], F32, tag="small")
+        warm_tensor_engine(nc, warm_bank, zeros, WARM_PASSES_EARLY)
+
         nc.vector.memset(w_ih_plane[:].bitcast(I32), 0)
         nc.vector.memset(table_warm[:], 0.0)
         nc.vector.memset(w_hh_plane[:].bitcast(I32), 0)
@@ -77,15 +85,17 @@ def tile_multilayerlstmcell_pa_s_kernel(
         load_scale_plane(nc, w_ih_plane, w_ih_scales)
         nc.scalar.dma_start(out=x_sb[:], in_=lstm_input)
         nc.scalar.dma_start(out=h_sb[:], in_=h_prev)
-        load_words(nc, w_ih_sb, w_ih_words, 0)
-        load_words(nc, w_hh_sb, w_hh_words, 0)
+        load_gate_words(nc, w_ih_sb, w_ih_words, gate_order[0])
+        load_gate_words(nc, w_hh_sb, w_hh_words, gate_order[0])
         load_scale_plane(nc, w_hh_plane, w_hh_scales)
-        load_words(nc, w_ih_sb, w_ih_words, 1)
-        load_words(nc, w_hh_sb, w_hh_words, 1)
+        for g in gate_order[1:]:
+            load_gate_words(nc, w_ih_sb, w_ih_words, g)
+            load_gate_words(nc, w_hh_sb, w_hh_words, g)
 
+        nc.gpsimd.memset(bias_rows[:], 0.0)
         nc.gpsimd.dma_start(out=bias_rows[0:16, :], in_=b_ih.rearrange("(m p) -> m p", p=P))
         nc.gpsimd.dma_start(out=bias_rows[16:32, :], in_=b_hh.rearrange("(m p) -> m p", p=P))
-        make_identity(nc, ident_f32[:], nomemset=True)
+        make_identity(nc, ident_f32[:])
         nc.gpsimd.dma_start(out=c_sb[:], in_=c_prev)
         nc.vector.tensor_copy(out=ident_bf16[:], in_=ident_f32[:])
 
@@ -95,6 +105,7 @@ def tile_multilayerlstmcell_pa_s_kernel(
         h_bank = psum_small.tile([P, 2, P], F32, tag="small")
         transpose_words(nc, x_bank, x_sb, ident_f32)
         transpose_words(nc, h_bank, h_sb, ident_f32)
+        warm_tensor_engine(nc, warm_bank, zeros, WARM_PASSES_GAP)
 
         x_grouped = keep.tile([P, P, 4], BF16, align_bytes=64)
         h_grouped = keep.tile([P, P, 4], BF16, align_bytes=64)
@@ -127,60 +138,53 @@ def tile_multilayerlstmcell_pa_s_kernel(
             op=ALU.add,
         )
 
+        gate_func = {GATE_I: ACT.Sigmoid, GATE_F: ACT.Sigmoid, GATE_G: ACT.Tanh, GATE_O: ACT.Sigmoid}
+        gate = {}
+        for g in gate_order:
+            acc = psum_gates.tile([P, BLOCKS, P], F32, tag="acc")
+            for j in range(BLOCKS):
+                m = g * BLOCKS + j
+                word_cols = slice(m * P * FP4_WORD_BYTES, (m + 1) * P * FP4_WORD_BYTES)
+                scale_cols = slice(m * P, (m + 1) * P)
+                nc.tensor.matmul_mx(
+                    out=acc[:, j, :],
+                    lhsT=w_ih_sb[:, word_cols].bitcast(FP4X4),
+                    lhsT_scale=w_ih_plane[:, scale_cols],
+                    rhs=x_codes[:].bitcast(FP8X4),
+                    rhs_scale=x_plane[:],
+                    start=True,
+                    stop=False,
+                )
+                nc.tensor.matmul_mx(
+                    out=acc[:, j, :],
+                    lhsT=w_hh_sb[:, word_cols].bitcast(FP4X4),
+                    lhsT_scale=w_hh_plane[:, scale_cols],
+                    rhs=h_codes[:].bitcast(FP8X4),
+                    rhs_scale=h_plane[:],
+                    start=False,
+                    stop=True,
+                )
+            gate[g] = keep.tile([P, BLOCKS, P], F32, name="gate%d" % g)
+            for j in range(BLOCKS):
+                m = g * BLOCKS + j
+                nc.scalar.activation(
+                    out=gate[g][:, j, :], in_=acc[:, j, :], func=gate_func[g], bias=bias[:, m : m + 1], scale=1.0
+                )
+
         def transpose_back(source_t, first, count):
             bank = psum_small.tile([P, count * P], F32, tag="small", name="back")
             for n in range(count):
                 nc.tensor.transpose(bank[:, n * P : (n + 1) * P], source_t[:, first + n, :], ident_f32[:])
             return bank
 
-        gate_func = {GATE_I: ACT.Sigmoid, GATE_F: ACT.Sigmoid, GATE_G: ACT.Tanh, GATE_O: ACT.Sigmoid}
-        gate = {}
-        forget_c = keep.tile([P, HIDDEN], F32)
-        for g in gate_order:
-            if g == GATE_O:
-                f_bank = transpose_back(gate[GATE_F], 0, BLOCKS)
-                nc.vector.tensor_tensor(out=forget_c[:], in0=f_bank[:], in1=c_sb[:], op=ALU.mult)
-            gate[g] = keep.tile([P, BLOCKS, P], F32, name="gate%d" % g)
-            for first in range(0, BLOCKS, BANK_BLOCKS):
-                acc = psum_gates.tile([P, BANK_BLOCKS, P], F32, tag="acc")
-                for n in range(BANK_BLOCKS):
-                    m = g * BLOCKS + first + n
-                    word_cols = slice(m * P * FP4_WORD_BYTES, (m + 1) * P * FP4_WORD_BYTES)
-                    scale_cols = slice(m * P, (m + 1) * P)
-                    nc.tensor.matmul_mx(
-                        out=acc[:, n, :],
-                        lhsT=w_ih_sb[:, word_cols].bitcast(FP4X4),
-                        lhsT_scale=w_ih_plane[:, scale_cols],
-                        rhs=x_codes[:].bitcast(FP8X4),
-                        rhs_scale=x_plane[:],
-                        start=True,
-                        stop=False,
-                    )
-                    nc.tensor.matmul_mx(
-                        out=acc[:, n, :],
-                        lhsT=w_hh_sb[:, word_cols].bitcast(FP4X4),
-                        lhsT_scale=w_hh_plane[:, scale_cols],
-                        rhs=h_codes[:].bitcast(FP8X4),
-                        rhs_scale=h_plane[:],
-                        start=False,
-                        stop=True,
-                    )
-                for n in range(BANK_BLOCKS):
-                    m = g * BLOCKS + first + n
-                    nc.scalar.activation(
-                        out=gate[g][:, first + n, :],
-                        in_=acc[:, n, :],
-                        func=gate_func[g],
-                        bias=bias[:, m : m + 1],
-                        scale=1.0,
-                    )
-
         input_g_t = keep.tile([P, BLOCKS, P], F32)
+        forget_c = keep.tile([P, HIDDEN], F32)
         c_next = keep.tile([P, HIDDEN], F32)
         tanh_c = keep.tile([P, HIDDEN], F32)
         h_next = keep.tile([P, HIDDEN], F32)
         chunk_starts = list(range(0, BLOCKS, TAIL_BLOCKS))
 
+        f_bank = transpose_back(gate[GATE_F], 0, BLOCKS)
         input_g_banks = []
         for first in chunk_starts:
             blocks = slice(first, first + TAIL_BLOCKS)
@@ -188,6 +192,7 @@ def tile_multilayerlstmcell_pa_s_kernel(
                 out=input_g_t[:, blocks, :], in0=gate[GATE_I][:, blocks, :], in1=gate[GATE_G][:, blocks, :], op=ALU.mult
             )
             input_g_banks.append(transpose_back(input_g_t, first, TAIL_BLOCKS))
+        nc.vector.tensor_tensor(out=forget_c[:], in0=f_bank[:], in1=c_sb[:], op=ALU.mult)
         for first, bank in zip(chunk_starts, input_g_banks):
             cols = slice(first * P, (first + TAIL_BLOCKS) * P)
             nc.vector.tensor_tensor(out=c_next[:, cols], in0=bank[:], in1=forget_c[:, cols], op=ALU.add)

@@ -19,23 +19,24 @@ GATES = 4
 BLOCKS = HIDDEN // P
 COLUMNS = GATES * HIDDEN
 FP4_WORD_BYTES = 2
+PSUM_BANKS = 8
+BANK_BLOCKS = 2
+TAIL_BLOCKS = 1
 WARM_PASSES_EARLY = 4
 WARM_PASSES_GAP = 2
-TAIL_BLOCKS = 2
 
 GATE_I, GATE_F, GATE_G, GATE_O = 0, 1, 2, 3
 
 FLOPS = 2 * P * (2 * HIDDEN) * COLUMNS
 
 
-def load_scale_plane(nc, plane, scales):
+def load_scale_rows(nc, plane, scales, r):
     rows = scales[0].rearrange("(quadrant r) n -> r quadrant n", r=4)
-    for r in range(4):
-        nc.sync.dma_start(out=plane[r:P:32, :].bitcast(I32), in_=rows[r].bitcast(I32))
+    nc.sync.dma_start(out=plane[r:P:32, :].bitcast(I32), in_=rows[r].bitcast(I32))
 
 
-def load_gate_words(nc, words_sb, words, g):
-    cols = slice(g * HIDDEN * FP4_WORD_BYTES, (g + 1) * HIDDEN * FP4_WORD_BYTES)
+def load_gate_words(nc, words_sb, words, first_gate, gates):
+    cols = slice(first_gate * HIDDEN * FP4_WORD_BYTES, (first_gate + gates) * HIDDEN * FP4_WORD_BYTES)
     nc.sync.dma_start(out=words_sb[:, cols].bitcast(I32), in_=words[0][:, cols].bitcast(I32))
 
 
@@ -57,8 +58,7 @@ def tile_multilayerlstmcell_pa_s_kernel(
     gate_order = (GATE_F, GATE_I, GATE_G, GATE_O)
     with ExitStack() as ctx:
         keep = ctx.enter_context(tc.tile_pool(name="keep", bufs=1))
-        psum_small = ctx.enter_context(tc.psum_pool(name="psum_small", bufs=4))
-        psum_gates = ctx.enter_context(tc.psum_pool(name="psum_gates", bufs=GATES))
+        psum = ctx.enter_context(tc.psum_pool(name="psum", bufs=PSUM_BANKS))
         ctx.enter_context(tc.manual_schedule())
 
         x_sb = keep.tile([P, HIDDEN], BF16)
@@ -75,34 +75,47 @@ def tile_multilayerlstmcell_pa_s_kernel(
         zeros = keep.tile([P, P], F32)
 
         nc.vector.memset(zeros[:], 0.0)
-        warm_bank = psum_small.tile([P, P], F32, tag="small")
+        warm_bank = psum.tile([P, P], F32, tag="bank")
         warm_tensor_engine(nc, warm_bank, zeros, WARM_PASSES_EARLY)
 
         nc.vector.memset(w_ih_plane[:].bitcast(I32), 0)
         nc.vector.memset(table_warm[:], 0.0)
         nc.vector.memset(w_hh_plane[:].bitcast(I32), 0)
+        nc.vector.memset(bias_rows[32:64, :], 0.0)
+        nc.vector.memset(bias_rows[64:128, :], 0.0)
+        make_identity(nc, ident_f32[:])
+        nc.vector.tensor_copy(out=ident_bf16[:], in_=ident_f32[:])
 
-        load_scale_plane(nc, w_ih_plane, w_ih_scales)
+        nc.scalar.dma_start(out=bias_rows[0:16, :], in_=b_ih.rearrange("(m p) -> m p", p=P))
+        nc.scalar.dma_start(out=bias_rows[16:32, :], in_=b_hh.rearrange("(m p) -> m p", p=P))
         nc.scalar.dma_start(out=x_sb[:], in_=lstm_input)
         nc.scalar.dma_start(out=h_sb[:], in_=h_prev)
-        load_gate_words(nc, w_ih_sb, w_ih_words, gate_order[0])
-        load_gate_words(nc, w_hh_sb, w_hh_words, gate_order[0])
-        load_scale_plane(nc, w_hh_plane, w_hh_scales)
-        for g in gate_order[1:]:
-            load_gate_words(nc, w_ih_sb, w_ih_words, g)
-            load_gate_words(nc, w_hh_sb, w_hh_words, g)
-
-        nc.gpsimd.memset(bias_rows[:], 0.0)
-        nc.gpsimd.dma_start(out=bias_rows[0:16, :], in_=b_ih.rearrange("(m p) -> m p", p=P))
-        nc.gpsimd.dma_start(out=bias_rows[16:32, :], in_=b_hh.rearrange("(m p) -> m p", p=P))
-        make_identity(nc, ident_f32[:])
+        load_scale_rows(nc, w_ih_plane, w_ih_scales, 0)
+        load_scale_rows(nc, w_ih_plane, w_ih_scales, 1)
+        load_gate_words(nc, w_ih_sb, w_ih_words, GATE_I, 2)
+        load_gate_words(nc, w_hh_sb, w_hh_words, GATE_I, 2)
+        load_scale_rows(nc, w_ih_plane, w_ih_scales, 2)
+        load_scale_rows(nc, w_ih_plane, w_ih_scales, 3)
+        for r in range(4):
+            load_scale_rows(nc, w_hh_plane, w_hh_scales, r)
+        load_gate_words(nc, w_ih_sb, w_ih_words, GATE_G, 2)
+        load_gate_words(nc, w_hh_sb, w_hh_words, GATE_G, 2)
         nc.gpsimd.dma_start(out=c_sb[:], in_=c_prev)
-        nc.vector.tensor_copy(out=ident_bf16[:], in_=ident_f32[:])
 
         nc.scalar.activation(out=table_warm[:, 1:2], in_=table_warm[:, 0:1], func=ACT.Sigmoid)
 
-        x_bank = psum_small.tile([P, 2, P], F32, tag="small")
-        h_bank = psum_small.tile([P, 2, P], F32, tag="small")
+        bias_bank = psum.tile([P, P], BF16, tag="bank")
+        nc.tensor.transpose(bias_bank[:], bias_rows[:], ident_bf16[:])
+        bias = keep.tile([P, GATES * BLOCKS], F32)
+        nc.vector.tensor_reduce(
+            out=bias[:],
+            in_=bias_bank[:, 0 : 2 * GATES * BLOCKS].rearrange("p (s m) -> p m s", s=2),
+            axis=mybir.AxisListType.X,
+            op=ALU.add,
+        )
+
+        x_bank = psum.tile([P, 2, P], F32, tag="bank")
+        h_bank = psum.tile([P, 2, P], F32, tag="bank")
         transpose_words(nc, x_bank, x_sb, ident_f32)
         transpose_words(nc, h_bank, h_sb, ident_f32)
         warm_tensor_engine(nc, warm_bank, zeros, WARM_PASSES_GAP)
@@ -128,51 +141,46 @@ def tile_multilayerlstmcell_pa_s_kernel(
             out=h_codes[:].bitcast(FP8X4), scales=h_plane[:], in_=h_grouped[:].rearrange("p b t -> p (b t)")
         )
 
-        bias_bank = psum_small.tile([P, P], BF16, tag="small")
-        nc.tensor.transpose(bias_bank[:], bias_rows[:], ident_bf16[:])
-        bias = keep.tile([P, GATES * BLOCKS], F32)
-        nc.vector.tensor_reduce(
-            out=bias[:],
-            in_=bias_bank[:, 0 : 2 * GATES * BLOCKS].rearrange("p (s m) -> p m s", s=2),
-            axis=mybir.AxisListType.X,
-            op=ALU.add,
-        )
-
         gate_func = {GATE_I: ACT.Sigmoid, GATE_F: ACT.Sigmoid, GATE_G: ACT.Tanh, GATE_O: ACT.Sigmoid}
         gate = {}
         for g in gate_order:
-            acc = psum_gates.tile([P, BLOCKS, P], F32, tag="acc")
-            for j in range(BLOCKS):
-                m = g * BLOCKS + j
-                word_cols = slice(m * P * FP4_WORD_BYTES, (m + 1) * P * FP4_WORD_BYTES)
-                scale_cols = slice(m * P, (m + 1) * P)
-                nc.tensor.matmul_mx(
-                    out=acc[:, j, :],
-                    lhsT=w_ih_sb[:, word_cols].bitcast(FP4X4),
-                    lhsT_scale=w_ih_plane[:, scale_cols],
-                    rhs=x_codes[:].bitcast(FP8X4),
-                    rhs_scale=x_plane[:],
-                    start=True,
-                    stop=False,
-                )
-                nc.tensor.matmul_mx(
-                    out=acc[:, j, :],
-                    lhsT=w_hh_sb[:, word_cols].bitcast(FP4X4),
-                    lhsT_scale=w_hh_plane[:, scale_cols],
-                    rhs=h_codes[:].bitcast(FP8X4),
-                    rhs_scale=h_plane[:],
-                    start=False,
-                    stop=True,
-                )
             gate[g] = keep.tile([P, BLOCKS, P], F32, name="gate%d" % g)
-            for j in range(BLOCKS):
-                m = g * BLOCKS + j
-                nc.scalar.activation(
-                    out=gate[g][:, j, :], in_=acc[:, j, :], func=gate_func[g], bias=bias[:, m : m + 1], scale=1.0
-                )
+            for first in range(0, BLOCKS, BANK_BLOCKS):
+                acc = psum.tile([P, BANK_BLOCKS, P], F32, tag="bank")
+                for n in range(BANK_BLOCKS):
+                    m = g * BLOCKS + first + n
+                    word_cols = slice(m * P * FP4_WORD_BYTES, (m + 1) * P * FP4_WORD_BYTES)
+                    scale_cols = slice(m * P, (m + 1) * P)
+                    nc.tensor.matmul_mx(
+                        out=acc[:, n, :],
+                        lhsT=w_ih_sb[:, word_cols].bitcast(FP4X4),
+                        lhsT_scale=w_ih_plane[:, scale_cols],
+                        rhs=x_codes[:].bitcast(FP8X4),
+                        rhs_scale=x_plane[:],
+                        start=True,
+                        stop=False,
+                    )
+                    nc.tensor.matmul_mx(
+                        out=acc[:, n, :],
+                        lhsT=w_hh_sb[:, word_cols].bitcast(FP4X4),
+                        lhsT_scale=w_hh_plane[:, scale_cols],
+                        rhs=h_codes[:].bitcast(FP8X4),
+                        rhs_scale=h_plane[:],
+                        start=False,
+                        stop=True,
+                    )
+                for n in range(BANK_BLOCKS):
+                    m = g * BLOCKS + first + n
+                    nc.scalar.activation(
+                        out=gate[g][:, first + n, :],
+                        in_=acc[:, n, :],
+                        func=gate_func[g],
+                        bias=bias[:, m : m + 1],
+                        scale=1.0,
+                    )
 
         def transpose_back(source_t, first, count):
-            bank = psum_small.tile([P, count * P], F32, tag="small", name="back")
+            bank = psum.tile([P, count * P], F32, tag="bank", name="back")
             for n in range(count):
                 nc.tensor.transpose(bank[:, n * P : (n + 1) * P], source_t[:, first + n, :], ident_f32[:])
             return bank

@@ -22,7 +22,7 @@ FP4_WORD_BYTES = 2
 PSUM_BANKS = 8
 BANK_BLOCKS = 2
 TAIL_BLOCKS = 1
-WARM_PASSES_EARLY = 4
+WARM_PASSES_EARLY = 6
 WARM_PASSES_GAP = 2
 
 GATE_I, GATE_F, GATE_G, GATE_O = 0, 1, 2, 3

@@ -55,7 +55,6 @@ def tile_multilayerlstmcell_pa_s_kernel(
     tc, lstm_input, h_prev, c_prev, w_ih_words, w_ih_scales, w_hh_words, w_hh_scales, b_ih, b_hh, out_0, out_1
 ):
     nc = tc.nc
-    gate_order = (GATE_F, GATE_I, GATE_G, GATE_O)
     with ExitStack() as ctx:
         keep = ctx.enter_context(tc.tile_pool(name="keep", bufs=1))
         psum = ctx.enter_context(tc.psum_pool(name="psum", bufs=PSUM_BANKS))
@@ -143,7 +142,8 @@ def tile_multilayerlstmcell_pa_s_kernel(
 
         gate_func = {GATE_I: ACT.Sigmoid, GATE_F: ACT.Sigmoid, GATE_G: ACT.Tanh, GATE_O: ACT.Sigmoid}
         gate = {}
-        for g in gate_order:
+
+        def run_gate(g):
             gate[g] = keep.tile([P, BLOCKS, P], F32, name="gate%d" % g)
             for first in range(0, BLOCKS, BANK_BLOCKS):
                 acc = psum.tile([P, BANK_BLOCKS, P], F32, tag="bank")
@@ -192,7 +192,12 @@ def tile_multilayerlstmcell_pa_s_kernel(
         h_next = keep.tile([P, HIDDEN], F32)
         chunk_starts = list(range(0, BLOCKS, TAIL_BLOCKS))
 
+        run_gate(GATE_F)
+        run_gate(GATE_I)
         f_bank = transpose_back(gate[GATE_F], 0, BLOCKS)
+        nc.vector.tensor_tensor(out=forget_c[:], in0=f_bank[:], in1=c_sb[:], op=ALU.mult)
+        run_gate(GATE_G)
+        run_gate(GATE_O)
         input_g_banks = []
         for first in chunk_starts:
             blocks = slice(first, first + TAIL_BLOCKS)
@@ -200,7 +205,6 @@ def tile_multilayerlstmcell_pa_s_kernel(
                 out=input_g_t[:, blocks, :], in0=gate[GATE_I][:, blocks, :], in1=gate[GATE_G][:, blocks, :], op=ALU.mult
             )
             input_g_banks.append(transpose_back(input_g_t, first, TAIL_BLOCKS))
-        nc.vector.tensor_tensor(out=forget_c[:], in0=f_bank[:], in1=c_sb[:], op=ALU.mult)
         for first, bank in zip(chunk_starts, input_g_banks):
             cols = slice(first * P, (first + TAIL_BLOCKS) * P)
             nc.vector.tensor_tensor(out=c_next[:, cols], in0=bank[:], in1=forget_c[:, cols], op=ALU.add)

@@ -143,41 +143,51 @@ def tile_multilayerlstmcell_pa_s_kernel(
         gate_func = {GATE_I: ACT.Sigmoid, GATE_F: ACT.Sigmoid, GATE_G: ACT.Tanh, GATE_O: ACT.Sigmoid}
         gate = {}
 
+        def gate_pass(acc, m, from_x):
+            word_cols = slice(m * P * FP4_WORD_BYTES, (m + 1) * P * FP4_WORD_BYTES)
+            scale_cols = slice(m * P, (m + 1) * P)
+            words_sb, plane, codes, codes_plane = (
+                (w_ih_sb, w_ih_plane, x_codes, x_plane) if from_x else (w_hh_sb, w_hh_plane, h_codes, h_plane)
+            )
+            nc.tensor.matmul_mx(
+                out=acc,
+                lhsT=words_sb[:, word_cols].bitcast(FP4X4),
+                lhsT_scale=plane[:, scale_cols],
+                rhs=codes[:].bitcast(FP8X4),
+                rhs_scale=codes_plane[:],
+                start=from_x,
+                stop=not from_x,
+            )
+
+        def activate(g, j, acc):
+            m = g * BLOCKS + j
+            nc.scalar.activation(
+                out=gate[g][:, j, :], in_=acc, func=gate_func[g], bias=bias[:, m : m + 1], scale=1.0
+            )
+
+        def open_gate(g):
+            gate[g] = keep.tile([P, BLOCKS, P], F32, name="gate%d" % g)
+            banks = []
+            for j in range(BLOCKS):
+                acc = psum.tile([P, P], F32, tag="bank", name="open")
+                gate_pass(acc[:], g * BLOCKS + j, True)
+                banks.append(acc)
+            return banks
+
+        def close_gate(g, banks):
+            for j in range(BLOCKS):
+                gate_pass(banks[j][:], g * BLOCKS + j, False)
+                activate(g, j, banks[j][:])
+
         def run_gate(g):
             gate[g] = keep.tile([P, BLOCKS, P], F32, name="gate%d" % g)
             for first in range(0, BLOCKS, BANK_BLOCKS):
                 acc = psum.tile([P, BANK_BLOCKS, P], F32, tag="bank")
                 for n in range(BANK_BLOCKS):
-                    m = g * BLOCKS + first + n
-                    word_cols = slice(m * P * FP4_WORD_BYTES, (m + 1) * P * FP4_WORD_BYTES)
-                    scale_cols = slice(m * P, (m + 1) * P)
-                    nc.tensor.matmul_mx(
-                        out=acc[:, n, :],
-                        lhsT=w_ih_sb[:, word_cols].bitcast(FP4X4),
-                        lhsT_scale=w_ih_plane[:, scale_cols],
-                        rhs=x_codes[:].bitcast(FP8X4),
-                        rhs_scale=x_plane[:],
-                        start=True,
-                        stop=False,
-                    )
-                    nc.tensor.matmul_mx(
-                        out=acc[:, n, :],
-                        lhsT=w_hh_sb[:, word_cols].bitcast(FP4X4),
-                        lhsT_scale=w_hh_plane[:, scale_cols],
-                        rhs=h_codes[:].bitcast(FP8X4),
-                        rhs_scale=h_plane[:],
-                        start=False,
-                        stop=True,
-                    )
+                    gate_pass(acc[:, n, :], g * BLOCKS + first + n, True)
+                    gate_pass(acc[:, n, :], g * BLOCKS + first + n, False)
                 for n in range(BANK_BLOCKS):
-                    m = g * BLOCKS + first + n
-                    nc.scalar.activation(
-                        out=gate[g][:, first + n, :],
-                        in_=acc[:, n, :],
-                        func=gate_func[g],
-                        bias=bias[:, m : m + 1],
-                        scale=1.0,
-                    )
+                    activate(g, first + n, acc[:, n, :])
 
         def transpose_back(source_t, first, count):
             bank = psum.tile([P, count * P], F32, tag="bank", name="back")
@@ -192,8 +202,10 @@ def tile_multilayerlstmcell_pa_s_kernel(
         h_next = keep.tile([P, HIDDEN], F32)
         chunk_starts = list(range(0, BLOCKS, TAIL_BLOCKS))
 
-        run_gate(GATE_F)
-        run_gate(GATE_I)
+        f_open = open_gate(GATE_F)
+        i_open = open_gate(GATE_I)
+        close_gate(GATE_F, f_open)
+        close_gate(GATE_I, i_open)
         f_bank = transpose_back(gate[GATE_F], 0, BLOCKS)
         nc.vector.tensor_tensor(out=forget_c[:], in0=f_bank[:], in1=c_sb[:], op=ALU.mult)
         run_gate(GATE_G)

@@ -22,7 +22,8 @@ FP4_WORD_BYTES = 2
 PSUM_BANKS = 8
 BANK_BLOCKS = 2
 TAIL_BLOCKS = 1
-WARM_PASSES_EARLY = 6
+TAIL_SPLIT = 2
+WARM_PASSES_EARLY = 3
 WARM_PASSES_GAP = 2
 
 GATE_I, GATE_F, GATE_G, GATE_O = 0, 1, 2, 3
@@ -218,12 +219,22 @@ def tile_multilayerlstmcell_pa_s_kernel(
             )
             input_g_banks.append(transpose_back(input_g_t, first, TAIL_BLOCKS))
         for first, bank in zip(chunk_starts, input_g_banks):
+            for half in range(TAIL_SPLIT):
+                width = TAIL_BLOCKS * P // TAIL_SPLIT
+                cols = slice(first * P + half * width, first * P + (half + 1) * width)
+                nc.vector.tensor_tensor(
+                    out=c_next[:, cols], in0=bank[:, half * width : (half + 1) * width], in1=forget_c[:, cols], op=ALU.add
+                )
+                nc.scalar.activation(out=tanh_c[:, cols], in_=c_next[:, cols], func=ACT.Tanh)
             cols = slice(first * P, (first + TAIL_BLOCKS) * P)
-            nc.vector.tensor_tensor(out=c_next[:, cols], in0=bank[:], in1=forget_c[:, cols], op=ALU.add)
             nc.sync.dma_start(out=out_1[:, cols], in_=c_next[:, cols])
-            nc.scalar.activation(out=tanh_c[:, cols], in_=c_next[:, cols], func=ACT.Tanh)
         for first in chunk_starts:
-            cols = slice(first * P, (first + TAIL_BLOCKS) * P)
             o_bank = transpose_back(gate[GATE_O], first, TAIL_BLOCKS)
-            nc.vector.tensor_tensor(out=h_next[:, cols], in0=o_bank[:], in1=tanh_c[:, cols], op=ALU.mult)
+            for half in range(TAIL_SPLIT):
+                width = TAIL_BLOCKS * P // TAIL_SPLIT
+                cols = slice(first * P + half * width, first * P + (half + 1) * width)
+                nc.vector.tensor_tensor(
+                    out=h_next[:, cols], in0=o_bank[:, half * width : (half + 1) * width], in1=tanh_c[:, cols], op=ALU.mult
+                )
+            cols = slice(first * P, (first + TAIL_BLOCKS) * P)
             nc.sync.dma_start(out=out_0[:, cols], in_=h_next[:, cols])

@@ -20,7 +20,7 @@ BLOCKS = HIDDEN // P
 COLUMNS = GATES * HIDDEN
 FP4_WORD_BYTES = 2
 PSUM_BANKS = 8
-BANK_BLOCKS = 2
+BANK_BLOCKS = 1
 TAIL_BLOCKS = 1
 TAIL_SPLIT = 2
 WARM_PASSES_EARLY = 3

@@ -74,11 +74,11 @@ def tile_multilayerlstmcell_pa_s_kernel(
         table_warm = keep.tile([P, 2], F32)
         zeros = keep.tile([P, P], F32)
 
-        nc.vector.memset(zeros[:], 0.0)
+        nc.vector.memset(w_ih_plane[:].bitcast(I32), 0)
+        nc.gpsimd.memset(zeros[:], 0.0)
         warm_bank = psum.tile([P, P], F32, tag="bank")
         warm_tensor_engine(nc, warm_bank, zeros, WARM_PASSES_EARLY)
 
-        nc.vector.memset(w_ih_plane[:].bitcast(I32), 0)
         nc.vector.memset(table_warm[:], 0.0)
         nc.vector.memset(w_hh_plane[:].bitcast(I32), 0)
         nc.vector.memset(bias_rows[32:64, :], 0.0)
@@ -86,9 +86,9 @@ def tile_multilayerlstmcell_pa_s_kernel(
         make_identity(nc, ident_f32[:])
         nc.vector.tensor_copy(out=ident_bf16[:], in_=ident_f32[:])
 
+        nc.scalar.dma_start(out=x_sb[:], in_=lstm_input)
         nc.scalar.dma_start(out=bias_rows[0:16, :], in_=b_ih.rearrange("(m p) -> m p", p=P))
         nc.scalar.dma_start(out=bias_rows[16:32, :], in_=b_hh.rearrange("(m p) -> m p", p=P))
-        nc.scalar.dma_start(out=x_sb[:], in_=lstm_input)
         nc.scalar.dma_start(out=h_sb[:], in_=h_prev)
         load_scale_rows(nc, w_ih_plane, w_ih_scales, 0)
         load_scale_rows(nc, w_ih_plane, w_ih_scales, 1)

@@ -20,9 +20,9 @@ BLOCKS = HIDDEN // P
 COLUMNS = GATES * HIDDEN
 FP4_WORD_BYTES = 2
 PSUM_BANKS = 8
-BANK_BLOCKS = 1
-TAIL_BLOCKS = 1
 TAIL_SPLIT = 2
+PAIR = 2
+EARLY_G = 3
 WARM_PASSES_EARLY = 3
 WARM_PASSES_GAP = 2
 
@@ -86,20 +86,19 @@ def tile_multilayerlstmcell_pa_s_kernel(
         make_identity(nc, ident_f32[:])
         nc.vector.tensor_copy(out=ident_bf16[:], in_=ident_f32[:])
 
-        nc.scalar.dma_start(out=x_sb[:], in_=lstm_input)
         nc.scalar.dma_start(out=bias_rows[0:16, :], in_=b_ih.rearrange("(m p) -> m p", p=P))
         nc.scalar.dma_start(out=bias_rows[16:32, :], in_=b_hh.rearrange("(m p) -> m p", p=P))
+        nc.scalar.dma_start(out=x_sb[:], in_=lstm_input)
         nc.scalar.dma_start(out=h_sb[:], in_=h_prev)
-        load_scale_rows(nc, w_ih_plane, w_ih_scales, 0)
-        load_scale_rows(nc, w_ih_plane, w_ih_scales, 1)
-        load_gate_words(nc, w_ih_sb, w_ih_words, GATE_I, 2)
-        load_gate_words(nc, w_hh_sb, w_hh_words, GATE_I, 2)
-        load_scale_rows(nc, w_ih_plane, w_ih_scales, 2)
+        for r in range(3):
+            load_scale_rows(nc, w_ih_plane, w_ih_scales, r)
+        load_gate_words(nc, w_ih_sb, w_ih_words, GATE_I, 3)
         load_scale_rows(nc, w_ih_plane, w_ih_scales, 3)
+        load_gate_words(nc, w_hh_sb, w_hh_words, GATE_I, 2)
         for r in range(4):
             load_scale_rows(nc, w_hh_plane, w_hh_scales, r)
-        load_gate_words(nc, w_ih_sb, w_ih_words, GATE_G, 2)
         load_gate_words(nc, w_hh_sb, w_hh_words, GATE_G, 2)
+        load_gate_words(nc, w_ih_sb, w_ih_words, GATE_O, 1)
         nc.gpsimd.dma_start(out=c_sb[:], in_=c_prev)
 
         nc.scalar.activation(out=table_warm[:, 1:2], in_=table_warm[:, 0:1], func=ACT.Sigmoid)
@@ -114,10 +113,28 @@ def tile_multilayerlstmcell_pa_s_kernel(
             op=ALU.add,
         )
 
+        selector = keep.tile([P, BLOCKS], BF16)
+        first_row = GATE_F * BLOCKS
+        nc.vector.tensor_tensor(
+            out=selector[:],
+            in0=ident_bf16[:, first_row : first_row + BLOCKS],
+            in1=ident_bf16[:, first_row + GATES * BLOCKS : first_row + (GATES + 1) * BLOCKS],
+            op=ALU.add,
+        )
         x_bank = psum.tile([P, 2, P], F32, tag="bank")
         h_bank = psum.tile([P, 2, P], F32, tag="bank")
         transpose_words(nc, x_bank, x_sb, ident_f32)
         transpose_words(nc, h_bank, h_sb, ident_f32)
+        bias_f_bank = psum.tile([P, HIDDEN], F32, tag="bank")
+        for j in range(BLOCKS):
+            nc.tensor.matmul(
+                out=bias_f_bank[:, j * P : (j + 1) * P],
+                lhsT=selector[:, j : j + 1].to_broadcast([P, P]),
+                rhs=bias_rows[:],
+                start=True,
+                stop=True,
+            )
+        bias_f = keep.tile([P, HIDDEN], F32)
         warm_tensor_engine(nc, warm_bank, zeros, WARM_PASSES_GAP)
 
         x_grouped = keep.tile([P, P, 4], BF16, align_bytes=64)
@@ -130,6 +147,7 @@ def tile_multilayerlstmcell_pa_s_kernel(
             out=h_grouped[:].rearrange("p b t -> p (b t)").bitcast(F32).rearrange("p (b u) -> p b u", u=2),
             in_=h_bank[:].rearrange("p u b -> p b u"),
         )
+        nc.scalar.copy(out=bias_f[:], in_=bias_f_bank[:])
         x_codes = keep.tile([P, P], U32, align_bytes=64)
         h_codes = keep.tile([P, P], U32, align_bytes=64)
         x_plane = keep.tile([P, P], U8, align_bytes=64)
@@ -141,100 +159,97 @@ def tile_multilayerlstmcell_pa_s_kernel(
             out=h_codes[:].bitcast(FP8X4), scales=h_plane[:], in_=h_grouped[:].rearrange("p b t -> p (b t)")
         )
 
-        gate_func = {GATE_I: ACT.Sigmoid, GATE_F: ACT.Sigmoid, GATE_G: ACT.Tanh, GATE_O: ACT.Sigmoid}
+        gate_func = {GATE_I: ACT.Sigmoid, GATE_G: ACT.Tanh, GATE_O: ACT.Sigmoid}
         gate = {}
-
-        def gate_pass(acc, m, from_x):
-            word_cols = slice(m * P * FP4_WORD_BYTES, (m + 1) * P * FP4_WORD_BYTES)
-            scale_cols = slice(m * P, (m + 1) * P)
-            words_sb, plane, codes, codes_plane = (
-                (w_ih_sb, w_ih_plane, x_codes, x_plane) if from_x else (w_hh_sb, w_hh_plane, h_codes, h_plane)
-            )
-            nc.tensor.matmul_mx(
-                out=acc,
-                lhsT=words_sb[:, word_cols].bitcast(FP4X4),
-                lhsT_scale=plane[:, scale_cols],
-                rhs=codes[:].bitcast(FP8X4),
-                rhs_scale=codes_plane[:],
-                start=from_x,
-                stop=not from_x,
-            )
-
-        def activate(g, j, acc):
-            m = g * BLOCKS + j
-            nc.scalar.activation(
-                out=gate[g][:, j, :], in_=acc, func=gate_func[g], bias=bias[:, m : m + 1], scale=1.0
-            )
-
-        def open_gate(g):
+        for g in (GATE_I, GATE_G, GATE_O):
             gate[g] = keep.tile([P, BLOCKS, P], F32, name="gate%d" % g)
-            banks = []
-            for j in range(BLOCKS):
-                acc = psum.tile([P, P], F32, tag="bank", name="open")
-                gate_pass(acc[:], g * BLOCKS + j, True)
-                banks.append(acc)
-            return banks
-
-        def close_gate(g, banks):
-            for j in range(BLOCKS):
-                gate_pass(banks[j][:], g * BLOCKS + j, False)
-                activate(g, j, banks[j][:])
-
-        def run_gate(g):
-            gate[g] = keep.tile([P, BLOCKS, P], F32, name="gate%d" % g)
-            for first in range(0, BLOCKS, BANK_BLOCKS):
-                acc = psum.tile([P, BANK_BLOCKS, P], F32, tag="bank")
-                for n in range(BANK_BLOCKS):
-                    gate_pass(acc[:, n, :], g * BLOCKS + first + n, True)
-                    gate_pass(acc[:, n, :], g * BLOCKS + first + n, False)
-                for n in range(BANK_BLOCKS):
-                    activate(g, first + n, acc[:, n, :])
-
-        def transpose_back(source_t, first, count):
-            bank = psum.tile([P, count * P], F32, tag="bank", name="back")
-            for n in range(count):
-                nc.tensor.transpose(bank[:, n * P : (n + 1) * P], source_t[:, first + n, :], ident_f32[:])
-            return bank
-
-        input_g_t = keep.tile([P, BLOCKS, P], F32)
+        f_sum = keep.tile([P, HIDDEN], F32)
+        f_gate = keep.tile([P, HIDDEN], F32)
         forget_c = keep.tile([P, HIDDEN], F32)
+        input_g_t = keep.tile([P, BLOCKS, P], F32)
         c_next = keep.tile([P, HIDDEN], F32)
         tanh_c = keep.tile([P, HIDDEN], F32)
         h_next = keep.tile([P, HIDDEN], F32)
-        chunk_starts = list(range(0, BLOCKS, TAIL_BLOCKS))
 
-        f_open = open_gate(GATE_F)
-        i_open = open_gate(GATE_I)
-        close_gate(GATE_F, f_open)
-        close_gate(GATE_I, i_open)
-        f_bank = transpose_back(gate[GATE_F], 0, BLOCKS)
-        nc.vector.tensor_tensor(out=forget_c[:], in0=f_bank[:], in1=c_sb[:], op=ALU.mult)
-        run_gate(GATE_G)
-        run_gate(GATE_O)
-        input_g_banks = []
-        for first in chunk_starts:
-            blocks = slice(first, first + TAIL_BLOCKS)
-            nc.vector.tensor_tensor(
-                out=input_g_t[:, blocks, :], in0=gate[GATE_I][:, blocks, :], in1=gate[GATE_G][:, blocks, :], op=ALU.mult
+        def operands(first, blocks, from_x):
+            word_cols = slice(first * P * FP4_WORD_BYTES, (first + blocks) * P * FP4_WORD_BYTES)
+            scale_cols = slice(first * P, (first + blocks) * P)
+            words_sb, plane, codes, codes_plane = (
+                (w_ih_sb, w_ih_plane, x_codes, x_plane) if from_x else (w_hh_sb, w_hh_plane, h_codes, h_plane)
             )
-            input_g_banks.append(transpose_back(input_g_t, first, TAIL_BLOCKS))
-        for first, bank in zip(chunk_starts, input_g_banks):
-            for half in range(TAIL_SPLIT):
-                width = TAIL_BLOCKS * P // TAIL_SPLIT
-                cols = slice(first * P + half * width, first * P + (half + 1) * width)
+            return words_sb[:, word_cols].bitcast(FP4X4), plane[:, scale_cols], codes[:].bitcast(FP8X4), codes_plane[:]
+
+        def gate_pass(acc, g, j, from_x):
+            words, scales, codes, codes_scales = operands(g * BLOCKS + j, 1, from_x)
+            nc.tensor.matmul_mx(
+                out=acc[:], lhsT=words, lhsT_scale=scales, rhs=codes, rhs_scale=codes_scales, start=from_x, stop=not from_x
+            )
+
+        def forget_pass(acc, from_x):
+            words, scales, codes, codes_scales = operands(GATE_F * BLOCKS, BLOCKS, from_x)
+            nc.tensor.matmul_mx(
+                out=acc[:], lhsT=codes, lhsT_scale=codes_scales, rhs=words, rhs_scale=scales, start=from_x, stop=not from_x
+            )
+
+        def open_block(g, j):
+            acc = psum.tile([P, P], F32, tag="bank", name="open")
+            gate_pass(acc, g, j, True)
+            return acc
+
+        def close_block(acc, g, j):
+            gate_pass(acc, g, j, False)
+            m = g * BLOCKS + j
+            nc.scalar.activation(
+                out=gate[g][:, j, :], in_=acc[:], func=gate_func[g], bias=bias[:, m : m + 1], scale=1.0
+            )
+
+        i_open = [open_block(GATE_I, j) for j in range(BLOCKS)]
+        g_open = [open_block(GATE_G, j) for j in range(EARLY_G)]
+        f_acc = psum.tile([P, HIDDEN], F32, tag="bank")
+        forget_pass(f_acc, True)
+        for j in range(BLOCKS):
+            close_block(i_open[j], GATE_I, j)
+        forget_pass(f_acc, False)
+        pairs = [slice(first * P, (first + PAIR) * P) for first in range(0, BLOCKS, PAIR)]
+        for cols in pairs:
+            nc.vector.tensor_tensor(out=f_sum[:, cols], in0=f_acc[:, cols], in1=bias_f[:, cols], op=ALU.add)
+        for j in range(BLOCKS):
+            close_block(g_open[j] if j < EARLY_G else open_block(GATE_G, j), GATE_G, j)
+            nc.vector.tensor_tensor(
+                out=input_g_t[:, j, :], in0=gate[GATE_I][:, j, :], in1=gate[GATE_G][:, j, :], op=ALU.mult
+            )
+        for cols in pairs:
+            nc.scalar.activation(out=f_gate[:, cols], in_=f_sum[:, cols], func=ACT.Sigmoid)
+            nc.vector.tensor_tensor(out=forget_c[:, cols], in0=f_gate[:, cols], in1=c_sb[:, cols], op=ALU.mult)
+        for j in range(BLOCKS):
+            close_block(open_block(GATE_O, j), GATE_O, j)
+
+        def transpose_back(source_t, j):
+            bank = psum.tile([P, P], F32, tag="bank", name="back")
+            nc.tensor.transpose(bank[:], source_t[:, j, :], ident_f32[:])
+            return bank
+
+        width = P // TAIL_SPLIT
+
+        def store(out, rows, j):
+            if j % PAIR == PAIR - 1:
+                cols = pairs[j // PAIR]
+                nc.sync.dma_start(out=out[:, cols], in_=rows[:, cols])
+
+        banks = [transpose_back(input_g_t, j) for j in range(BLOCKS)]
+        for j in range(BLOCKS):
+            for s in range(TAIL_SPLIT):
+                cols = slice(j * P + s * width, j * P + (s + 1) * width)
                 nc.vector.tensor_tensor(
-                    out=c_next[:, cols], in0=bank[:, half * width : (half + 1) * width], in1=forget_c[:, cols], op=ALU.add
+                    out=c_next[:, cols], in0=banks[j][:, s * width : (s + 1) * width], in1=forget_c[:, cols], op=ALU.add
                 )
                 nc.scalar.activation(out=tanh_c[:, cols], in_=c_next[:, cols], func=ACT.Tanh)
-            cols = slice(first * P, (first + TAIL_BLOCKS) * P)
-            nc.sync.dma_start(out=out_1[:, cols], in_=c_next[:, cols])
-        for first in chunk_starts:
-            o_bank = transpose_back(gate[GATE_O], first, TAIL_BLOCKS)
-            for half in range(TAIL_SPLIT):
-                width = TAIL_BLOCKS * P // TAIL_SPLIT
-                cols = slice(first * P + half * width, first * P + (half + 1) * width)
+            store(out_1, c_next, j)
+        for j in range(BLOCKS):
+            bank = transpose_back(gate[GATE_O], j)
+            for s in range(TAIL_SPLIT):
+                cols = slice(j * P + s * width, j * P + (s + 1) * width)
                 nc.vector.tensor_tensor(
-                    out=h_next[:, cols], in0=o_bank[:, half * width : (half + 1) * width], in1=tanh_c[:, cols], op=ALU.mult
+                    out=h_next[:, cols], in0=bank[:, s * width : (s + 1) * width], in1=tanh_c[:, cols], op=ALU.mult
                 )
-            cols = slice(first * P, (first + TAIL_BLOCKS) * P)
-            nc.sync.dma_start(out=out_0[:, cols], in_=h_next[:, cols])
+            store(out_0, h_next, j)

@@ -20,7 +20,7 @@ BLOCKS = HIDDEN // P
 COLUMNS = GATES * HIDDEN
 FP4_WORD_BYTES = 2
 PSUM_BANKS = 8
-TAIL_SPLIT = 2
+TAIL_SPLIT = 1
 PAIR = 2
 EARLY_G = 3
 WARM_PASSES_EARLY = 3
@@ -99,7 +99,7 @@ def tile_multilayerlstmcell_pa_s_kernel(
             load_scale_rows(nc, w_hh_plane, w_hh_scales, r)
         load_gate_words(nc, w_hh_sb, w_hh_words, GATE_G, 2)
         load_gate_words(nc, w_ih_sb, w_ih_words, GATE_O, 1)
-        nc.gpsimd.dma_start(out=c_sb[:], in_=c_prev)
+        nc.sync.dma_start(out=c_sb[:], in_=c_prev)
 
         nc.scalar.activation(out=table_warm[:, 1:2], in_=table_warm[:, 0:1], func=ACT.Sigmoid)
 
@@ -231,10 +231,9 @@ def tile_multilayerlstmcell_pa_s_kernel(
 
         width = P // TAIL_SPLIT
 
-        def store(out, rows, j):
-            if j % PAIR == PAIR - 1:
-                cols = pairs[j // PAIR]
-                nc.sync.dma_start(out=out[:, cols], in_=rows[:, cols])
+        def store(out, rows, first, count):
+            cols = slice(first * P, (first + count) * P)
+            nc.sync.dma_start(out=out[:, cols], in_=rows[:, cols])
 
         banks = [transpose_back(input_g_t, j) for j in range(BLOCKS)]
         for j in range(BLOCKS):
@@ -244,7 +243,7 @@ def tile_multilayerlstmcell_pa_s_kernel(
                     out=c_next[:, cols], in0=banks[j][:, s * width : (s + 1) * width], in1=forget_c[:, cols], op=ALU.add
                 )
                 nc.scalar.activation(out=tanh_c[:, cols], in_=c_next[:, cols], func=ACT.Tanh)
-            store(out_1, c_next, j)
+            store(out_1, c_next, j, 1)
         for j in range(BLOCKS):
             bank = transpose_back(gate[GATE_O], j)
             for s in range(TAIL_SPLIT):
@@ -252,4 +251,7 @@ def tile_multilayerlstmcell_pa_s_kernel(
                 nc.vector.tensor_tensor(
                     out=h_next[:, cols], in0=bank[:, s * width : (s + 1) * width], in1=tanh_c[:, cols], op=ALU.mult
                 )
-            store(out_0, h_next, j)
+            if j == PAIR - 1:
+                store(out_0, h_next, 0, PAIR)
+            elif j >= PAIR:
+                store(out_0, h_next, j, 1)

@@ -22,6 +22,7 @@ FP4_WORD_BYTES = 2
 PSUM_BANKS = 8
 TAIL_SPLIT = 1
 PAIR = 2
+FORGET_AFTER = 3
 EARLY_G = 3
 WARM_PASSES_EARLY = 3
 WARM_PASSES_GAP = 2
@@ -97,7 +98,8 @@ def tile_multilayerlstmcell_pa_s_kernel(
         load_gate_words(nc, w_hh_sb, w_hh_words, GATE_I, 2)
         for r in range(4):
             load_scale_rows(nc, w_hh_plane, w_hh_scales, r)
-        load_gate_words(nc, w_hh_sb, w_hh_words, GATE_G, 2)
+        load_gate_words(nc, w_hh_sb, w_hh_words, GATE_G, 1)
+        load_gate_words(nc, w_hh_sb, w_hh_words, GATE_O, 1)
         load_gate_words(nc, w_ih_sb, w_ih_words, GATE_O, 1)
         nc.sync.dma_start(out=c_sb[:], in_=c_prev)
 
@@ -208,8 +210,9 @@ def tile_multilayerlstmcell_pa_s_kernel(
         f_acc = psum.tile([P, HIDDEN], F32, tag="bank")
         forget_pass(f_acc, True)
         for j in range(BLOCKS):
+            if j == FORGET_AFTER:
+                forget_pass(f_acc, False)
             close_block(i_open[j], GATE_I, j)
-        forget_pass(f_acc, False)
         pairs = [slice(first * P, (first + PAIR) * P) for first in range(0, BLOCKS, PAIR)]
         for cols in pairs:
             nc.vector.tensor_tensor(out=f_sum[:, cols], in0=f_acc[:, cols], in1=bias_f[:, cols], op=ALU.add)
@@ -251,7 +254,5 @@ def tile_multilayerlstmcell_pa_s_kernel(
                 nc.vector.tensor_tensor(
                     out=h_next[:, cols], in0=bank[:, s * width : (s + 1) * width], in1=tanh_c[:, cols], op=ALU.mult
                 )
-            if j == PAIR - 1:
-                store(out_0, h_next, 0, PAIR)
-            elif j >= PAIR:
-                store(out_0, h_next, j, 1)
+            if j % PAIR == PAIR - 1:
+                store(out_0, h_next, j + 1 - PAIR, PAIR)

@@ -23,8 +23,7 @@ PSUM_BANKS = 8
 TAIL_SPLIT = 1
 PAIR = 2
 FORGET_AFTER = 3
-EARLY_G = 3
-WARM_PASSES_EARLY = 3
+WARM_PASSES_EARLY = 4
 WARM_PASSES_GAP = 2
 
 GATE_I, GATE_F, GATE_G, GATE_O = 0, 1, 2, 3
@@ -93,14 +92,14 @@ def tile_multilayerlstmcell_pa_s_kernel(
         nc.scalar.dma_start(out=h_sb[:], in_=h_prev)
         for r in range(3):
             load_scale_rows(nc, w_ih_plane, w_ih_scales, r)
-        load_gate_words(nc, w_ih_sb, w_ih_words, GATE_I, 3)
+        load_gate_words(nc, w_ih_sb, w_ih_words, GATE_I, 2)
         load_scale_rows(nc, w_ih_plane, w_ih_scales, 3)
         load_gate_words(nc, w_hh_sb, w_hh_words, GATE_I, 2)
         for r in range(4):
             load_scale_rows(nc, w_hh_plane, w_hh_scales, r)
-        load_gate_words(nc, w_hh_sb, w_hh_words, GATE_G, 1)
-        load_gate_words(nc, w_hh_sb, w_hh_words, GATE_O, 1)
-        load_gate_words(nc, w_ih_sb, w_ih_words, GATE_O, 1)
+        for g in (GATE_G, GATE_O):
+            load_gate_words(nc, w_ih_sb, w_ih_words, g, 1)
+            load_gate_words(nc, w_hh_sb, w_hh_words, g, 1)
         nc.sync.dma_start(out=c_sb[:], in_=c_prev)
 
         nc.scalar.activation(out=table_warm[:, 1:2], in_=table_warm[:, 0:1], func=ACT.Sigmoid)
@@ -206,7 +205,6 @@ def tile_multilayerlstmcell_pa_s_kernel(
             )
 
         i_open = [open_block(GATE_I, j) for j in range(BLOCKS)]
-        g_open = [open_block(GATE_G, j) for j in range(EARLY_G)]
         f_acc = psum.tile([P, HIDDEN], F32, tag="bank")
         forget_pass(f_acc, True)
         for j in range(BLOCKS):
@@ -217,7 +215,7 @@ def tile_multilayerlstmcell_pa_s_kernel(
         for cols in pairs:
             nc.vector.tensor_tensor(out=f_sum[:, cols], in0=f_acc[:, cols], in1=bias_f[:, cols], op=ALU.add)
         for j in range(BLOCKS):
-            close_block(g_open[j] if j < EARLY_G else open_block(GATE_G, j), GATE_G, j)
+            close_block(open_block(GATE_G, j), GATE_G, j)
             nc.vector.tensor_tensor(
                 out=input_g_t[:, j, :], in0=gate[GATE_I][:, j, :], in1=gate[GATE_G][:, j, :], op=ALU.mult
             )
@@ -246,7 +244,10 @@ def tile_multilayerlstmcell_pa_s_kernel(
                     out=c_next[:, cols], in0=banks[j][:, s * width : (s + 1) * width], in1=forget_c[:, cols], op=ALU.add
                 )
                 nc.scalar.activation(out=tanh_c[:, cols], in_=c_next[:, cols], func=ACT.Tanh)
-            store(out_1, c_next, j, 1)
+            if j == PAIR - 1:
+                store(out_1, c_next, 0, PAIR)
+            elif j >= PAIR:
+                store(out_1, c_next, j, 1)
         for j in range(BLOCKS):
             bank = transpose_back(gate[GATE_O], j)
             for s in range(TAIL_SPLIT):

from contextlib import ExitStack

import concourse.mybir as mybir
from concourse.masks import make_identity

F32 = mybir.dt.float32
BF16 = mybir.dt.bfloat16
I32 = mybir.dt.int32
U32 = mybir.dt.uint32
U8 = mybir.dt.uint8
FP8X4 = mybir.dt.float8_e4m3fn_x4
FP4X4 = mybir.dt.float4_e2m1fn_x4
ACT = mybir.ActivationFunctionType
ALU = mybir.AluOpType

P = 128
HIDDEN = 512
GATES = 4
BLOCKS = HIDDEN // P
COLUMNS = GATES * HIDDEN
FP4_WORD_BYTES = 2
PSUM_BANKS = 8
TAIL_SPLIT = 1
PAIR = 2
FORGET_AFTER = 3
WARM_PASSES_EARLY = 4
WARM_PASSES_GAP = 2

GATE_I, GATE_F, GATE_G, GATE_O = 0, 1, 2, 3

FLOPS = 2 * P * (2 * HIDDEN) * COLUMNS


def load_scale_rows(nc, plane, scales, r):
    rows = scales[0].rearrange("(quadrant r) n -> r quadrant n", r=4)
    nc.sync.dma_start(out=plane[r:P:32, :].bitcast(I32), in_=rows[r].bitcast(I32))


def load_gate_words(nc, words_sb, words, first_gate, gates):
    cols = slice(first_gate * HIDDEN * FP4_WORD_BYTES, (first_gate + gates) * HIDDEN * FP4_WORD_BYTES)
    nc.sync.dma_start(out=words_sb[:, cols].bitcast(I32), in_=words[0][:, cols].bitcast(I32))


def warm_tensor_engine(nc, bank, zeros, passes):
    for n in range(passes):
        nc.tensor.matmul(out=bank[:], lhsT=zeros[:], rhs=zeros[:], start=True, stop=True)


def transpose_words(nc, bank, rows_sb, ident_f32):
    words = rows_sb[:].bitcast(F32)
    for u in range(2):
        nc.tensor.transpose(bank[:, u, :], words[:, u : HIDDEN // 2 : 2], ident_f32[:])


def tile_multilayerlstmcell_pa_s_kernel(
    tc, lstm_input, h_prev, c_prev, w_ih_words, w_ih_scales, w_hh_words, w_hh_scales, b_ih, b_hh, out_0, out_1
):
    nc = tc.nc
    with ExitStack() as ctx:
        keep = ctx.enter_context(tc.tile_pool(name="keep", bufs=1))
        psum = ctx.enter_context(tc.psum_pool(name="psum", bufs=PSUM_BANKS))
        ctx.enter_context(tc.manual_schedule())

        x_sb = keep.tile([P, HIDDEN], BF16)
        h_sb = keep.tile([P, HIDDEN], BF16)
        c_sb = keep.tile([P, HIDDEN], BF16)
        w_ih_sb = keep.tile([P, COLUMNS * FP4_WORD_BYTES], U8, align_bytes=64)
        w_hh_sb = keep.tile([P, COLUMNS * FP4_WORD_BYTES], U8, align_bytes=64)
        w_ih_plane = keep.tile([P, COLUMNS], U8, align_bytes=64)
        w_hh_plane = keep.tile([P, COLUMNS], U8, align_bytes=64)
        bias_rows = keep.tile([P, P], BF16)
        ident_f32 = keep.tile([P, P], F32)
        ident_bf16 = keep.tile([P, P], BF16)
        table_warm = keep.tile([P, 2], F32)
        zeros = keep.tile([P, P], F32)

        nc.vector.memset(w_ih_plane[:].bitcast(I32), 0)
        nc.gpsimd.memset(zeros[:], 0.0)
        warm_bank = psum.tile([P, P], F32, tag="bank")
        warm_tensor_engine(nc, warm_bank, zeros, WARM_PASSES_EARLY)

        nc.vector.memset(table_warm[:], 0.0)
        nc.vector.memset(w_hh_plane[:].bitcast(I32), 0)
        nc.vector.memset(bias_rows[32:64, :], 0.0)
        nc.vector.memset(bias_rows[64:128, :], 0.0)
        make_identity(nc, ident_f32[:])
        nc.vector.tensor_copy(out=ident_bf16[:], in_=ident_f32[:])

        nc.scalar.dma_start(out=bias_rows[0:16, :], in_=b_ih.rearrange("(m p) -> m p", p=P))
        nc.scalar.dma_start(out=bias_rows[16:32, :], in_=b_hh.rearrange("(m p) -> m p", p=P))
        nc.scalar.dma_start(out=x_sb[:], in_=lstm_input)
        nc.scalar.dma_start(out=h_sb[:], in_=h_prev)
        for r in range(3):
            load_scale_rows(nc, w_ih_plane, w_ih_scales, r)
        load_gate_words(nc, w_ih_sb, w_ih_words, GATE_I, 2)
        load_scale_rows(nc, w_ih_plane, w_ih_scales, 3)
        load_gate_words(nc, w_hh_sb, w_hh_words, GATE_I, 2)
        for r in range(4):
            load_scale_rows(nc, w_hh_plane, w_hh_scales, r)
        for g in (GATE_G, GATE_O):
            load_gate_words(nc, w_ih_sb, w_ih_words, g, 1)
            load_gate_words(nc, w_hh_sb, w_hh_words, g, 1)
        nc.sync.dma_start(out=c_sb[:], in_=c_prev)

        nc.scalar.activation(out=table_warm[:, 1:2], in_=table_warm[:, 0:1], func=ACT.Sigmoid)

        bias_bank = psum.tile([P, P], BF16, tag="bank")
        nc.tensor.transpose(bias_bank[:], bias_rows[:], ident_bf16[:])
        bias = keep.tile([P, GATES * BLOCKS], F32)
        nc.vector.tensor_reduce(
            out=bias[:],
            in_=bias_bank[:, 0 : 2 * GATES * BLOCKS].rearrange("p (s m) -> p m s", s=2),
            axis=mybir.AxisListType.X,
            op=ALU.add,
        )

        selector = keep.tile([P, BLOCKS], BF16)
        first_row = GATE_F * BLOCKS
        nc.vector.tensor_tensor(
            out=selector[:],
            in0=ident_bf16[:, first_row : first_row + BLOCKS],
            in1=ident_bf16[:, first_row + GATES * BLOCKS : first_row + (GATES + 1) * BLOCKS],
            op=ALU.add,
        )
        x_bank = psum.tile([P, 2, P], F32, tag="bank")
        h_bank = psum.tile([P, 2, P], F32, tag="bank")
        transpose_words(nc, x_bank, x_sb, ident_f32)
        transpose_words(nc, h_bank, h_sb, ident_f32)
        bias_f_bank = psum.tile([P, HIDDEN], F32, tag="bank")
        for j in range(BLOCKS):
            nc.tensor.matmul(
                out=bias_f_bank[:, j * P : (j + 1) * P],
                lhsT=selector[:, j : j + 1].to_broadcast([P, P]),
                rhs=bias_rows[:],
                start=True,
                stop=True,
            )
        bias_f = keep.tile([P, HIDDEN], F32)
        warm_tensor_engine(nc, warm_bank, zeros, WARM_PASSES_GAP)

        x_grouped = keep.tile([P, P, 4], BF16, align_bytes=64)
        h_grouped = keep.tile([P, P, 4], BF16, align_bytes=64)
        nc.vector.tensor_copy(
            out=x_grouped[:].rearrange("p b t -> p (b t)").bitcast(F32).rearrange("p (b u) -> p b u", u=2),
            in_=x_bank[:].rearrange("p u b -> p b u"),
        )
        nc.scalar.copy(
            out=h_grouped[:].rearrange("p b t -> p (b t)").bitcast(F32).rearrange("p (b u) -> p b u", u=2),
            in_=h_bank[:].rearrange("p u b -> p b u"),
        )
        nc.scalar.copy(out=bias_f[:], in_=bias_f_bank[:])
        x_codes = keep.tile([P, P], U32, align_bytes=64)
        h_codes = keep.tile([P, P], U32, align_bytes=64)
        x_plane = keep.tile([P, P], U8, align_bytes=64)
        h_plane = keep.tile([P, P], U8, align_bytes=64)
        nc.vector.quantize_mx(
            out=x_codes[:].bitcast(FP8X4), scales=x_plane[:], in_=x_grouped[:].rearrange("p b t -> p (b t)")
        )
        nc.vector.quantize_mx(
            out=h_codes[:].bitcast(FP8X4), scales=h_plane[:], in_=h_grouped[:].rearrange("p b t -> p (b t)")
        )

        gate_func = {GATE_I: ACT.Sigmoid, GATE_G: ACT.Tanh, GATE_O: ACT.Sigmoid}
        gate = {}
        for g in (GATE_I, GATE_G, GATE_O):
            gate[g] = keep.tile([P, BLOCKS, P], F32, name="gate%d" % g)
        f_sum = keep.tile([P, HIDDEN], F32)
        f_gate = keep.tile([P, HIDDEN], F32)
        forget_c = keep.tile([P, HIDDEN], F32)
        input_g_t = keep.tile([P, BLOCKS, P], F32)
        c_next = keep.tile([P, HIDDEN], F32)
        tanh_c = keep.tile([P, HIDDEN], F32)
        h_next = keep.tile([P, HIDDEN], F32)

        def operands(first, blocks, from_x):
            word_cols = slice(first * P * FP4_WORD_BYTES, (first + blocks) * P * FP4_WORD_BYTES)
            scale_cols = slice(first * P, (first + blocks) * P)
            words_sb, plane, codes, codes_plane = (
                (w_ih_sb, w_ih_plane, x_codes, x_plane) if from_x else (w_hh_sb, w_hh_plane, h_codes, h_plane)
            )
            return words_sb[:, word_cols].bitcast(FP4X4), plane[:, scale_cols], codes[:].bitcast(FP8X4), codes_plane[:]

        def gate_pass(acc, g, j, from_x):
            words, scales, codes, codes_scales = operands(g * BLOCKS + j, 1, from_x)
            nc.tensor.matmul_mx(
                out=acc[:], lhsT=words, lhsT_scale=scales, rhs=codes, rhs_scale=codes_scales, start=from_x, stop=not from_x
            )

        def forget_pass(acc, from_x):
            words, scales, codes, codes_scales = operands(GATE_F * BLOCKS, BLOCKS, from_x)
            nc.tensor.matmul_mx(
                out=acc[:], lhsT=codes, lhsT_scale=codes_scales, rhs=words, rhs_scale=scales, start=from_x, stop=not from_x
            )

        def open_block(g, j):
            acc = psum.tile([P, P], F32, tag="bank", name="open")
            gate_pass(acc, g, j, True)
            return acc

        def close_block(acc, g, j):
            gate_pass(acc, g, j, False)
            m = g * BLOCKS + j
            nc.scalar.activation(
                out=gate[g][:, j, :], in_=acc[:], func=gate_func[g], bias=bias[:, m : m + 1], scale=1.0
            )

        i_open = [open_block(GATE_I, j) for j in range(BLOCKS)]
        f_acc = psum.tile([P, HIDDEN], F32, tag="bank")
        forget_pass(f_acc, True)
        for j in range(BLOCKS):
            if j == FORGET_AFTER:
                forget_pass(f_acc, False)
            close_block(i_open[j], GATE_I, j)
        pairs = [slice(first * P, (first + PAIR) * P) for first in range(0, BLOCKS, PAIR)]
        for cols in pairs:
            nc.vector.tensor_tensor(out=f_sum[:, cols], in0=f_acc[:, cols], in1=bias_f[:, cols], op=ALU.add)
        for j in range(BLOCKS):
            close_block(open_block(GATE_G, j), GATE_G, j)
            nc.vector.tensor_tensor(
                out=input_g_t[:, j, :], in0=gate[GATE_I][:, j, :], in1=gate[GATE_G][:, j, :], op=ALU.mult
            )
        for cols in pairs:
            nc.scalar.activation(out=f_gate[:, cols], in_=f_sum[:, cols], func=ACT.Sigmoid)
            nc.vector.tensor_tensor(out=forget_c[:, cols], in0=f_gate[:, cols], in1=c_sb[:, cols], op=ALU.mult)
        for j in range(BLOCKS):
            close_block(open_block(GATE_O, j), GATE_O, j)

        def transpose_back(source_t, j):
            bank = psum.tile([P, P], F32, tag="bank", name="back")
            nc.tensor.transpose(bank[:], source_t[:, j, :], ident_f32[:])
            return bank

        width = P // TAIL_SPLIT

        def store(out, rows, first, count):
            cols = slice(first * P, (first + count) * P)
            nc.sync.dma_start(out=out[:, cols], in_=rows[:, cols])

        banks = [transpose_back(input_g_t, j) for j in range(BLOCKS)]
        for j in range(BLOCKS):
            for s in range(TAIL_SPLIT):
                cols = slice(j * P + s * width, j * P + (s + 1) * width)
                nc.vector.tensor_tensor(
                    out=c_next[:, cols], in0=banks[j][:, s * width : (s + 1) * width], in1=forget_c[:, cols], op=ALU.add
                )
                nc.scalar.activation(out=tanh_c[:, cols], in_=c_next[:, cols], func=ACT.Tanh)
            if j == PAIR - 1:
                store(out_1, c_next, 0, PAIR)
            elif j >= PAIR:
                store(out_1, c_next, j, 1)
        for j in range(BLOCKS):
            bank = transpose_back(gate[GATE_O], j)
            for s in range(TAIL_SPLIT):
                cols = slice(j * P + s * width, j * P + (s + 1) * width)
                nc.vector.tensor_tensor(
                    out=h_next[:, cols], in0=bank[:, s * width : (s + 1) * width], in1=tanh_c[:, cols], op=ALU.mult
                )
            if j % PAIR == PAIR - 1:
                store(out_0, h_next, j + 1 - PAIR, PAIR)
